import numpy as np
import ml_dtypes


def mxq(x, axis, fmt="e4m3"):
    dtype, down = {"e4m3": (ml_dtypes.float8_e4m3fn, 7), "e5m2": (ml_dtypes.float8_e5m2, 14)}[fmt]
    v = np.moveaxis(np.asarray(x, np.float32).astype(ml_dtypes.bfloat16).astype(np.float64), axis, -1)
    blocks = v.reshape(v.shape[:-1] + (-1, 32))
    amax = np.abs(blocks).max(-1, keepdims=True)
    byte = np.maximum(np.where(amax > 0, np.frexp(amax)[1] - 1 + 127, 0) - down, 1)
    scale = np.exp2(byte - 127.0)
    codes = (blocks / scale).astype(np.float32).astype(dtype).astype(np.float64)
    return np.moveaxis((codes * scale).reshape(v.shape), -1, axis)


WIDE = False


def mx_kscale(k):
    if not WIDE:
        return np.ones(k)
    levels = np.array([10, -10, 5, -5, 0])
    a = np.random.permutation(np.resize(levels, k // 512 * 4)).reshape(k // 512, 4)
    idx = np.arange(k)
    return np.exp2(a[idx // 512, idx % 128 // 32])


BF16 = ml_dtypes.bfloat16


def bf(x):
    return np.asarray(x, np.float32).astype(BF16)


def f64(x):
    return np.asarray(x).astype(np.float64)


B, NR, NQ, D, H, F = 4, 1024, 2048, 2, 256, 512
C = H + H
LN_EPS = 1e-5


def setup_inputs():
    s, t = mx_kscale(C), mx_kscale(F)
    return {"pq": bf(np.random.standard_normal((B, NQ, H)) * s[:H]),
            "attended": bf(np.random.standard_normal((B, NQ, H)) * s[H:]),
            "Wf1": bf(np.random.standard_normal((C, F)) / np.sqrt(C) / s[:, None] * t),
            "bf1": bf(np.random.standard_normal(F) * 0.2 * t),
            "Wf2": bf(np.random.standard_normal((F, H)) * 1.5 / np.sqrt(F) / t[:, None]),
            "bf2": bf(np.random.standard_normal(H) * 0.3),
            "ln_g": bf(1.0 + 0.1 * np.random.standard_normal(H)),
            "ln_b": bf(0.1 * np.random.standard_normal(H))}


def reference(pq, attended, Wf1, bf1, Wf2, bf2, ln_g, ln_b):
    final_inp = np.concatenate([f64(pq), f64(attended)], axis=2)
    h = np.maximum((mxq(final_inp, 2, "e4m3") @ mxq(f64(Wf1), 0, "e4m3")) + f64(bf1), 0.0)
    y = (mxq(h, 2, "e4m3") @ mxq(f64(Wf2), 0, "e4m3")) + f64(bf2)
    mu = np.mean(y, axis=-1, keepdims=True)
    var = np.mean(np.square(y - mu), axis=-1, keepdims=True)
    return (y - mu) / np.sqrt(var + LN_EPS) * f64(ln_g) + f64(ln_b)

@@ -1,0 +1,311 @@
+from contextlib import ExitStack
+
+import concourse.mybir as mybir
+from concourse.masks import make_identity
+
+F32 = mybir.dt.float32
+BF16 = mybir.dt.bfloat16
+U32 = mybir.dt.uint32
+U8 = mybir.dt.uint8
+FP8X4 = mybir.dt.float8_e4m3fn_x4
+ALU = mybir.AluOpType
+ACT = mybir.ActivationFunctionType
+
+P = 128
+PACK = 4
+TOKENS = 4 * 2048
+H = 256
+C = 2 * H
+F = 512
+BLOCK = 512
+TILES = BLOCK // P
+N_BLOCKS = TOKENS // BLOCK
+BANK = 512
+LN_EPS = 1e-5
+SCALAR_TOKENS = 192
+VECTOR_TOKENS = BLOCK - SCALAR_TOKENS
+
+FLOPS = 2 * TOKENS * C * F + 2 * TOKENS * F * H
+
+
+def tile_spatialattentionlayer_pb_t_kernel(
+    tc, pq, attended, Wf1, bf1, Wf2, bf2, ln_g, ln_b, out
+):
+    nc = tc.nc
+    pq_blocks = pq.rearrange("b (n p r) h -> (b n) p (r h)", p=P, r=TILES)
+    att_blocks = attended.rearrange("b (n p r) h -> (b n) p (r h)", p=P, r=TILES)
+    out_blocks = out.rearrange("b (n p r) j -> (b n) p (r j)", p=P, r=TILES)
+
+    with ExitStack() as ctx:
+        const = ctx.enter_context(tc.tile_pool(name="const", bufs=1))
+        xin = ctx.enter_context(tc.tile_pool(name="xin", bufs=N_BLOCKS))
+        work = ctx.enter_context(tc.tile_pool(name="work", bufs=3))
+        res = ctx.enter_context(tc.tile_pool(name="res", bufs=3))
+        ps_x = ctx.enter_context(tc.psum_pool(name="ps_x", bufs=2))
+        ps_h = ctx.enter_context(tc.psum_pool(name="ps_h", bufs=4))
+        ps_y = ctx.enter_context(tc.psum_pool(name="ps_y", bufs=2))
+        ctx.enter_context(tc.manual_schedule())
+
+        w1_raw = const.tile([P, PACK, F], BF16)
+        for u in range(2):
+            nc.sync.dma_start(
+                out=w1_raw[:, 2 * u : 2 * u + 2, :],
+                in_=Wf1[H * u : H * (u + 1), :].rearrange("(q e) f -> q e f", e=2),
+            )
+        pq_tiles = {}
+        att_tiles = {}
+
+        def load_block(b):
+            pq_sb = xin.tile([P, TILES * H], BF16)
+            nc.sync.dma_start(out=pq_sb[:], in_=pq_blocks[b])
+            att_sb = xin.tile([P, TILES * H], BF16)
+            nc.sync.dma_start(out=att_sb[:], in_=att_blocks[b])
+            pq_tiles[b] = pq_sb
+            att_tiles[b] = att_sb
+
+        load_block(0)
+        b1_bf = const.tile([P, PACK], BF16)
+        nc.sync.dma_start(out=b1_bf[:], in_=bf1.rearrange("(p t) -> p t", t=PACK))
+        w2_raw = const.tile([P, PACK, H], BF16)
+        nc.sync.dma_start(out=w2_raw[:], in_=Wf2.rearrange("(p t) j -> p t j", t=PACK))
+        load_block(1)
+        b2_rows = const.tile([P, H], BF16)
+        nc.sync.dma_start(out=b2_rows[:], in_=bf2.partition_broadcast(P))
+        g_rows = const.tile([P, H], BF16)
+        nc.sync.dma_start(out=g_rows[:], in_=ln_g.partition_broadcast(P))
+        b_rows = const.tile([P, H], BF16)
+        nc.sync.dma_start(out=b_rows[:], in_=ln_b.partition_broadcast(P))
+        for b in range(2, N_BLOCKS):
+            load_block(b)
+
+        ident = const.tile([P, P], F32)
+        make_identity(nc, ident[:])
+        eps = const.tile([P, 1], F32)
+        nc.vector.memset(eps[:], LN_EPS)
+        b1 = const.tile([P, PACK], F32)
+        nc.vector.tensor_copy(out=b1[:], in_=b1_bf[:])
+
+        w1_grouped = const.tile([P, F, PACK], BF16, align_bytes=64)
+        nc.vector.tensor_copy(
+            out=w1_grouped[:].rearrange("q (t m) s -> q t m s", t=PACK),
+            in_=w1_raw[:].rearrange("q s (m t) -> q t m s", t=PACK),
+        )
+        w1_codes = const.tile([P, F], U32, align_bytes=64)
+        w1_scales = const.tile([P, F], U8, align_bytes=64)
+        nc.vector.quantize_mx(
+            out=w1_codes[:].bitcast(FP8X4),
+            scales=w1_scales[:],
+            in_=w1_grouped[:].rearrange("q f s -> q (f s)"),
+        )
+        w2_grouped = const.tile([P, H, PACK], BF16, align_bytes=64)
+        nc.vector.tensor_copy(out=w2_grouped[:], in_=w2_raw[:].rearrange("p t j -> p j t"))
+        w2_codes = const.tile([P, H], U32, align_bytes=64)
+        w2_scales = const.tile([P, H], U8, align_bytes=64)
+        nc.vector.quantize_mx(
+            out=w2_codes[:].bitcast(FP8X4),
+            scales=w2_scales[:],
+            in_=w2_grouped[:].rearrange("p j t -> p (j t)"),
+        )
+
+        xt_tiles = {}
+        cg_tiles = {}
+        c_mx = {}
+        h_banks = {}
+        h_planes = {}
+        hg_tiles = {}
+        h_mx = {}
+        y_banks = {}
+        z_tiles = {}
+        stats = {}
+
+        def transpose_c(b):
+            for half in range(2):
+                xt = ps_x.tile([P, BANK], F32)
+                for r2 in range(2):
+                    r = 2 * half + r2
+                    for u, src in enumerate((pq_tiles[b], att_tiles[b])):
+                        col = (2 * r2 + u) * P
+                        nc.tensor.transpose(
+                            xt[:, col : col + P],
+                            src[:].bitcast(F32)[:, r * P : (r + 1) * P],
+                            ident[:],
+                        )
+                xt_tiles[(b, half)] = xt
+
+        def copy_c(b):
+            cg = work.tile([P, BLOCK * PACK], BF16, align_bytes=64)
+            cg_words = cg[:].bitcast(F32)
+            for half in range(2):
+                nc.scalar.copy(
+                    out=cg_words[:, half * BANK : (half + 1) * BANK].rearrange(
+                        "q (r w u) -> q r w u", r=2, u=2
+                    ),
+                    in_=xt_tiles[(b, half)][:].rearrange("q (r u w) -> q r w u", r=2, u=2),
+                )
+            cg_tiles[b] = cg
+
+        def quantise_c(b):
+            c_codes = work.tile([P, BLOCK], U32, align_bytes=64)
+            c_scales = work.tile([P, BLOCK], U8, align_bytes=64)
+            nc.vector.quantize_mx(
+                out=c_codes[:].bitcast(FP8X4), scales=c_scales[:], in_=cg_tiles[b][:]
+            )
+            c_mx[b] = (c_codes, c_scales)
+
+        def first_product(b):
+            c_codes, c_scales = c_mx[b]
+            for t in range(PACK):
+                h_ps = ps_h.tile([P, BLOCK], F32)
+                nc.tensor.matmul_mx(
+                    out=h_ps[:],
+                    lhsT=w1_codes[:, t * P : (t + 1) * P].bitcast(FP8X4),
+                    lhsT_scale=w1_scales[:, t * P : (t + 1) * P],
+                    rhs=c_codes[:].bitcast(FP8X4),
+                    rhs_scale=c_scales[:],
+                    start=True,
+                    stop=True,
+                )
+                h_banks[(b, t)] = h_ps
+
+        def relu_h(b):
+            h_plane = work.tile([P, PACK, BLOCK], BF16)
+            for t in range(PACK):
+                nc.scalar.activation(
+                    out=h_plane[:, t, :],
+                    in_=h_banks[(b, t)][:],
+                    func=ACT.Relu,
+                    bias=b1[:, t : t + 1],
+                    scale=1.0,
+                )
+            h_planes[b] = h_plane
+
+        def regroup_h_scalar(b):
+            hg = work.tile([P, BLOCK, PACK], BF16, align_bytes=64)
+            nc.scalar.copy(
+                out=hg[:, VECTOR_TOKENS:, :].rearrange("p (c i) t -> p c t i", i=4),
+                in_=h_planes[b][:, :, VECTOR_TOKENS:].rearrange("p t (c i) -> p c t i", i=4),
+            )
+            hg_tiles[b] = hg
+
+        def regroup_h_vector(b):
+            nc.vector.tensor_copy(
+                out=hg_tiles[b][:, :VECTOR_TOKENS, :].rearrange("p (c i) t -> p c t i", i=4),
+                in_=h_planes[b][:, :, :VECTOR_TOKENS].rearrange("p t (c i) -> p c t i", i=4),
+            )
+
+        def quantise_h(b):
+            h_codes = work.tile([P, BLOCK], U32, align_bytes=64)
+            h_scales = work.tile([P, BLOCK], U8, align_bytes=64)
+            nc.vector.quantize_mx(
+                out=h_codes[:].bitcast(FP8X4),
+                scales=h_scales[:],
+                in_=hg_tiles[b][:].rearrange("p n t -> p (n t)"),
+            )
+            h_mx[b] = (h_codes, h_scales)
+
+        def second_product(b):
+            h_codes, h_scales = h_mx[b]
+            for half in range(2):
+                y_ps = ps_y.tile([P, 2, H], F32)
+                for r2 in range(2):
+                    r = 2 * half + r2
+                    nc.tensor.matmul_mx(
+                        out=y_ps[:, r2, :],
+                        lhsT=h_codes[:, r * P : (r + 1) * P].bitcast(FP8X4),
+                        lhsT_scale=h_scales[:, r * P : (r + 1) * P],
+                        rhs=w2_codes[:].bitcast(FP8X4),
+                        rhs_scale=w2_scales[:],
+                        start=True,
+                        stop=True,
+                    )
+                y_banks[(b, half)] = y_ps
+
+        def add_bias_and_mean(b):
+            z = work.tile([P, TILES, H], F32)
+            z_sum = work.tile([P, TILES], F32)
+            for r in range(TILES):
+                nc.vector.scalar_tensor_tensor(
+                    out=z[:, r, :],
+                    in0=y_banks[(b, r // 2)][:, r % 2, :],
+                    scalar=1.0,
+                    in1=b2_rows[:],
+                    op0=ALU.mult,
+                    op1=ALU.add,
+                    accum_out=z_sum[:, r : r + 1],
+                )
+            neg_mean = work.tile([P, TILES], F32)
+            nc.vector.tensor_scalar_mul(out=neg_mean[:], in0=z_sum[:], scalar1=-1.0 / H)
+            z_tiles[b] = z
+            stats[(b, "neg_mean")] = neg_mean
+
+        def deviation(b):
+            neg_mean = stats[(b, "neg_mean")]
+            sq_sum = work.tile([P, TILES], F32)
+            for r in range(TILES):
+                squares = work.tile([P, H], F32)
+                nc.scalar.activation(
+                    out=squares[:],
+                    in_=z_tiles[b][:, r, :],
+                    func=ACT.Square,
+                    bias=neg_mean[:, r : r + 1],
+                    scale=1.0,
+                    accum_out=sq_sum[:, r : r + 1],
+                )
+            std = work.tile([P, TILES], F32)
+            nc.scalar.activation(
+                out=std[:], in_=sq_sum[:], func=ACT.Sqrt, bias=eps[:, 0:1], scale=1.0 / H
+            )
+            stats[(b, "std")] = std
+
+        def normalise_and_store(b):
+            neg_mean = stats[(b, "neg_mean")]
+            o = res.tile([P, TILES, H], F32)
+            for r in range(TILES):
+                nc.vector.scalar_tensor_tensor(
+                    out=o[:, r, :],
+                    in0=z_tiles[b][:, r, :],
+                    scalar=neg_mean[:, r : r + 1],
+                    in1=g_rows[:],
+                    op0=ALU.add,
+                    op1=ALU.mult,
+                )
+            rstd = work.tile([P, TILES], F32)
+            nc.vector.reciprocal(out=rstd[:], in_=stats[(b, "std")][:])
+            for r in range(TILES):
+                nc.vector.scalar_tensor_tensor(
+                    out=o[:, r, :],
+                    in0=o[:, r, :],
+                    scalar=rstd[:, r : r + 1],
+                    in1=b_rows[:],
+                    op0=ALU.mult,
+                    op1=ALU.add,
+                )
+            nc.sync.dma_start(out=out_blocks[b], in_=o[:].rearrange("p r j -> p (r j)"))
+
+        def in_range(b):
+            return 0 <= b < N_BLOCKS
+
+        for i in range(-2, N_BLOCKS + 3):
+            if in_range(i + 2):
+                transpose_c(i + 2)
+            if in_range(i - 2):
+                add_bias_and_mean(i - 2)
+            if in_range(i - 3):
+                deviation(i - 3)
+            if in_range(i - 1):
+                regroup_h_vector(i - 1)
+            if in_range(i + 1):
+                quantise_c(i + 1)
+            if in_range(i):
+                relu_h(i)
+            if in_range(i + 1):
+                first_product(i + 1)
+            if in_range(i):
+                regroup_h_scalar(i)
+            if in_range(i - 1):
+                quantise_h(i - 1)
+                second_product(i - 1)
+            if in_range(i + 2):
+                copy_c(i + 2)
+            if in_range(i - 3):
+                normalise_and_store(i - 3)

@@ -288,12 +288,15 @@ def tile_spatialattentionlayer_pb_t_kernel(
         for i in range(-2, N_BLOCKS + 3):
             if in_range(i + 2):
                 transpose_c(i + 2)
+            if in_range(i - 1):
+                regroup_h_vector(i - 1)
             if in_range(i - 2):
                 add_bias_and_mean(i - 2)
             if in_range(i - 3):
                 deviation(i - 3)
             if in_range(i - 1):
-                regroup_h_vector(i - 1)
+                quantise_h(i - 1)
+                second_product(i - 1)
             if in_range(i + 1):
                 quantise_c(i + 1)
             if in_range(i):
@@ -302,9 +305,6 @@ def tile_spatialattentionlayer_pb_t_kernel(
                 first_product(i + 1)
             if in_range(i):
                 regroup_h_scalar(i)
-            if in_range(i - 1):
-                quantise_h(i - 1)
-                second_product(i - 1)
             if in_range(i + 2):
                 copy_c(i + 2)
             if in_range(i - 3):

@@ -22,7 +22,7 @@ TILES = BLOCK // P
 N_BLOCKS = TOKENS // BLOCK
 BANK = 512
 LN_EPS = 1e-5
-SCALAR_TOKENS = 192
+SCALAR_TOKENS = 256
 VECTOR_TOKENS = BLOCK - SCALAR_TOKENS
 
 FLOPS = 2 * TOKENS * C * F + 2 * TOKENS * F * H
@@ -82,8 +82,6 @@ def tile_spatialattentionlayer_pb_t_kernel(
         make_identity(nc, ident[:])
         eps = const.tile([P, 1], F32)
         nc.vector.memset(eps[:], LN_EPS)
-        b1 = const.tile([P, PACK], F32)
-        nc.vector.tensor_copy(out=b1[:], in_=b1_bf[:])
 
         w1_grouped = const.tile([P, F, PACK], BF16, align_bytes=64)
         nc.vector.tensor_copy(
@@ -97,6 +95,8 @@ def tile_spatialattentionlayer_pb_t_kernel(
             scales=w1_scales[:],
             in_=w1_grouped[:].rearrange("q f s -> q (f s)"),
         )
+        b1 = const.tile([P, PACK], F32)
+        nc.vector.tensor_copy(out=b1[:], in_=b1_bf[:])
         w2_grouped = const.tile([P, H, PACK], BF16, align_bytes=64)
         nc.vector.tensor_copy(out=w2_grouped[:], in_=w2_raw[:].rearrange("p t j -> p j t"))
         w2_codes = const.tile([P, H], U32, align_bytes=64)
@@ -220,7 +220,7 @@ def tile_spatialattentionlayer_pb_t_kernel(
                     )
                 y_banks[(b, half)] = y_ps
 
-        def add_bias_and_mean(b):
+        def add_bias(b):
             z = work.tile([P, TILES, H], F32)
             z_sum = work.tile([P, TILES], F32)
             for r in range(TILES):
@@ -233,12 +233,15 @@ def tile_spatialattentionlayer_pb_t_kernel(
                     op1=ALU.add,
                     accum_out=z_sum[:, r : r + 1],
                 )
-            neg_mean = work.tile([P, TILES], F32)
-            nc.vector.tensor_scalar_mul(out=neg_mean[:], in0=z_sum[:], scalar1=-1.0 / H)
             z_tiles[b] = z
+            stats[(b, "z_sum")] = z_sum
+
+        def mean(b):
+            neg_mean = work.tile([P, TILES], F32)
+            nc.scalar.mul(out=neg_mean[:], in_=stats[(b, "z_sum")][:], mul=-1.0 / H)
             stats[(b, "neg_mean")] = neg_mean
 
-        def deviation(b):
+        def square_sums(b):
             neg_mean = stats[(b, "neg_mean")]
             sq_sum = work.tile([P, TILES], F32)
             for r in range(TILES):
@@ -251,14 +254,22 @@ def tile_spatialattentionlayer_pb_t_kernel(
                     scale=1.0,
                     accum_out=sq_sum[:, r : r + 1],
                 )
-            std = work.tile([P, TILES], F32)
+            stats[(b, "sq_sum")] = sq_sum
+
+        def inverse_deviation(b):
+            rstd = work.tile([P, TILES], F32)
             nc.scalar.activation(
-                out=std[:], in_=sq_sum[:], func=ACT.Sqrt, bias=eps[:, 0:1], scale=1.0 / H
+                out=rstd[:],
+                in_=stats[(b, "sq_sum")][:],
+                func=ACT.Abs_reciprocal_sqrt,
+                bias=eps[:, 0:1],
+                scale=1.0 / H,
             )
-            stats[(b, "std")] = std
+            stats[(b, "rstd")] = rstd
 
         def normalise_and_store(b):
             neg_mean = stats[(b, "neg_mean")]
+            rstd = stats[(b, "rstd")]
             o = res.tile([P, TILES, H], F32)
             for r in range(TILES):
                 nc.vector.scalar_tensor_tensor(
@@ -269,8 +280,6 @@ def tile_spatialattentionlayer_pb_t_kernel(
                     op0=ALU.add,
                     op1=ALU.mult,
                 )
-            rstd = work.tile([P, TILES], F32)
-            nc.vector.reciprocal(out=rstd[:], in_=stats[(b, "std")][:])
             for r in range(TILES):
                 nc.vector.scalar_tensor_tensor(
                     out=o[:, r, :],
@@ -291,9 +300,9 @@ def tile_spatialattentionlayer_pb_t_kernel(
             if in_range(i - 1):
                 regroup_h_vector(i - 1)
             if in_range(i - 2):
-                add_bias_and_mean(i - 2)
+                add_bias(i - 2)
             if in_range(i - 3):
-                deviation(i - 3)
+                square_sums(i - 3)
             if in_range(i - 1):
                 quantise_h(i - 1)
                 second_product(i - 1)
@@ -303,8 +312,12 @@ def tile_spatialattentionlayer_pb_t_kernel(
                 relu_h(i)
             if in_range(i + 1):
                 first_product(i + 1)
+            if in_range(i - 3):
+                inverse_deviation(i - 3)
             if in_range(i):
                 regroup_h_scalar(i)
+            if in_range(i - 2):
+                mean(i - 2)
             if in_range(i + 2):
                 copy_c(i + 2)
             if in_range(i - 3):

@@ -22,7 +22,7 @@ TILES = BLOCK // P
 N_BLOCKS = TOKENS // BLOCK
 BANK = 512
 LN_EPS = 1e-5
-SCALAR_TOKENS = 256
+SCALAR_TOKENS = 128
 VECTOR_TOKENS = BLOCK - SCALAR_TOKENS
 
 FLOPS = 2 * TOKENS * C * F + 2 * TOKENS * F * H
@@ -39,12 +39,11 @@ def tile_spatialattentionlayer_pb_t_kernel(
     with ExitStack() as ctx:
         const = ctx.enter_context(tc.tile_pool(name="const", bufs=1))
         xin = ctx.enter_context(tc.tile_pool(name="xin", bufs=N_BLOCKS))
-        work = ctx.enter_context(tc.tile_pool(name="work", bufs=3))
+        work = ctx.enter_context(tc.tile_pool(name="work", bufs=4))
         res = ctx.enter_context(tc.tile_pool(name="res", bufs=3))
         ps_x = ctx.enter_context(tc.psum_pool(name="ps_x", bufs=2))
         ps_h = ctx.enter_context(tc.psum_pool(name="ps_h", bufs=4))
         ps_y = ctx.enter_context(tc.psum_pool(name="ps_y", bufs=2))
-        ctx.enter_context(tc.manual_schedule())
 
         w1_raw = const.tile([P, PACK, F], BF16)
         for u in range(2):

@@ -22,7 +22,7 @@ TILES = BLOCK // P
 N_BLOCKS = TOKENS // BLOCK
 BANK = 512
 LN_EPS = 1e-5
-SCALAR_TOKENS = 128
+SCALAR_TOKENS = 160
 VECTOR_TOKENS = BLOCK - SCALAR_TOKENS
 
 FLOPS = 2 * TOKENS * C * F + 2 * TOKENS * F * H
@@ -34,7 +34,7 @@ def tile_spatialattentionlayer_pb_t_kernel(
     nc = tc.nc
     pq_blocks = pq.rearrange("b (n p r) h -> (b n) p (r h)", p=P, r=TILES)
     att_blocks = attended.rearrange("b (n p r) h -> (b n) p (r h)", p=P, r=TILES)
-    out_blocks = out.rearrange("b (n p r) j -> (b n) p (r j)", p=P, r=TILES)
+    out_blocks = out.rearrange("b (n p r) j -> (b n) p r j", p=P, r=TILES)
 
     with ExitStack() as ctx:
         const = ctx.enter_context(tc.tile_pool(name="const", bufs=1))
@@ -44,6 +44,7 @@ def tile_spatialattentionlayer_pb_t_kernel(
         ps_x = ctx.enter_context(tc.psum_pool(name="ps_x", bufs=2))
         ps_h = ctx.enter_context(tc.psum_pool(name="ps_h", bufs=4))
         ps_y = ctx.enter_context(tc.psum_pool(name="ps_y", bufs=2))
+        ctx.enter_context(tc.manual_schedule())
 
         w1_raw = const.tile([P, PACK, F], BF16)
         for u in range(2):
@@ -288,7 +289,7 @@ def tile_spatialattentionlayer_pb_t_kernel(
                     op0=ALU.mult,
                     op1=ALU.add,
                 )
-            nc.sync.dma_start(out=out_blocks[b], in_=o[:].rearrange("p r j -> p (r j)"))
+                nc.sync.dma_start(out=out_blocks[b][:, r, :], in_=o[:, r, :])
 
         def in_range(b):
             return 0 <= b < N_BLOCKS

@@ -17,13 +17,14 @@ TOKENS = 4 * 2048
 H = 256
 C = 2 * H
 F = 512
-BLOCK = 512
-TILES = BLOCK // P
-N_BLOCKS = TOKENS // BLOCK
 BANK = 512
 LN_EPS = 1e-5
-SCALAR_TOKENS = 160
-VECTOR_TOKENS = BLOCK - SCALAR_TOKENS
+BLOCK = 512
+N_BLOCKS = TOKENS // BLOCK
+SIZES = (BLOCK,) * N_BLOCKS
+STARTS = tuple(BLOCK * b for b in range(N_BLOCKS))
+GPSIMD_TOKENS = 192
+SCALAR_TOKENS = (0,) * 5 + (64,) * (N_BLOCKS - 8) + (320,) * 3
 
 FLOPS = 2 * TOKENS * C * F + 2 * TOKENS * F * H
 
@@ -32,13 +33,12 @@ def tile_spatialattentionlayer_pb_t_kernel(
     tc, pq, attended, Wf1, bf1, Wf2, bf2, ln_g, ln_b, out
 ):
     nc = tc.nc
-    pq_blocks = pq.rearrange("b (n p r) h -> (b n) p (r h)", p=P, r=TILES)
-    att_blocks = attended.rearrange("b (n p r) h -> (b n) p (r h)", p=P, r=TILES)
-    out_blocks = out.rearrange("b (n p r) j -> (b n) p r j", p=P, r=TILES)
+    pq_rows = pq.rearrange("b n h -> (b n) h")
+    att_rows = attended.rearrange("b n h -> (b n) h")
+    out_rows = out.rearrange("b n h -> (b n) h")
 
     with ExitStack() as ctx:
         const = ctx.enter_context(tc.tile_pool(name="const", bufs=1))
-        xin = ctx.enter_context(tc.tile_pool(name="xin", bufs=N_BLOCKS))
         work = ctx.enter_context(tc.tile_pool(name="work", bufs=4))
         res = ctx.enter_context(tc.tile_pool(name="res", bufs=3))
         ps_x = ctx.enter_context(tc.psum_pool(name="ps_x", bufs=2))
@@ -46,42 +46,50 @@ def tile_spatialattentionlayer_pb_t_kernel(
         ps_y = ctx.enter_context(tc.psum_pool(name="ps_y", bufs=2))
         ctx.enter_context(tc.manual_schedule())
 
+        pq_all = const.tile([P, TOKENS // P * H], BF16)
+        att_all = const.tile([P, TOKENS // P * H], BF16)
+
+        def columns(b):
+            return slice(STARTS[b] // P * H, (STARTS[b] + SIZES[b]) // P * H)
+
+        def load_block(b):
+            rows = slice(STARTS[b], STARTS[b] + SIZES[b])
+            for sb, hbm in ((pq_all, pq_rows), (att_all, att_rows)):
+                nc.sync.dma_start(
+                    out=sb[:, columns(b)], in_=hbm[rows, :].rearrange("(p r) h -> p (r h)", p=P)
+                )
+
         w1_raw = const.tile([P, PACK, F], BF16)
         for u in range(2):
             nc.sync.dma_start(
                 out=w1_raw[:, 2 * u : 2 * u + 2, :],
                 in_=Wf1[H * u : H * (u + 1), :].rearrange("(q e) f -> q e f", e=2),
             )
-        pq_tiles = {}
-        att_tiles = {}
-
-        def load_block(b):
-            pq_sb = xin.tile([P, TILES * H], BF16)
-            nc.sync.dma_start(out=pq_sb[:], in_=pq_blocks[b])
-            att_sb = xin.tile([P, TILES * H], BF16)
-            nc.sync.dma_start(out=att_sb[:], in_=att_blocks[b])
-            pq_tiles[b] = pq_sb
-            att_tiles[b] = att_sb
-
         load_block(0)
+        load_block(1)
         b1_bf = const.tile([P, PACK], BF16)
         nc.sync.dma_start(out=b1_bf[:], in_=bf1.rearrange("(p t) -> p t", t=PACK))
         w2_raw = const.tile([P, PACK, H], BF16)
         nc.sync.dma_start(out=w2_raw[:], in_=Wf2.rearrange("(p t) j -> p t j", t=PACK))
-        load_block(1)
+        load_block(2)
+        load_block(3)
         b2_rows = const.tile([P, H], BF16)
         nc.sync.dma_start(out=b2_rows[:], in_=bf2.partition_broadcast(P))
         g_rows = const.tile([P, H], BF16)
         nc.sync.dma_start(out=g_rows[:], in_=ln_g.partition_broadcast(P))
         b_rows = const.tile([P, H], BF16)
         nc.sync.dma_start(out=b_rows[:], in_=ln_b.partition_broadcast(P))
-        for b in range(2, N_BLOCKS):
+        for b in range(4, N_BLOCKS):
             load_block(b)
 
         ident = const.tile([P, P], F32)
         make_identity(nc, ident[:])
         eps = const.tile([P, 1], F32)
         nc.vector.memset(eps[:], LN_EPS)
+        first_use = const.tile([P, 1], F32)
+        nc.scalar.activation(
+            out=first_use[:], in_=eps[:], func=ACT.Abs_reciprocal_sqrt, bias=eps[:, 0:1], scale=1.0
+        )
 
         w1_grouped = const.tile([P, F, PACK], BF16, align_bytes=64)
         nc.vector.tensor_copy(
@@ -96,16 +104,17 @@ def tile_spatialattentionlayer_pb_t_kernel(
             in_=w1_grouped[:].rearrange("q f s -> q (f s)"),
         )
         b1 = const.tile([P, PACK], F32)
-        nc.vector.tensor_copy(out=b1[:], in_=b1_bf[:])
         w2_grouped = const.tile([P, H, PACK], BF16, align_bytes=64)
-        nc.vector.tensor_copy(out=w2_grouped[:], in_=w2_raw[:].rearrange("p t j -> p j t"))
         w2_codes = const.tile([P, H], U32, align_bytes=64)
         w2_scales = const.tile([P, H], U8, align_bytes=64)
-        nc.vector.quantize_mx(
-            out=w2_codes[:].bitcast(FP8X4),
-            scales=w2_scales[:],
-            in_=w2_grouped[:].rearrange("p j t -> p (j t)"),
-        )
+
+        def prepare_w2():
+            nc.vector.tensor_copy(out=w2_grouped[:], in_=w2_raw[:].rearrange("p t j -> p j t"))
+            nc.vector.quantize_mx(
+                out=w2_codes[:].bitcast(FP8X4),
+                scales=w2_scales[:],
+                in_=w2_grouped[:].rearrange("p j t -> p (j t)"),
+            )
 
         xt_tiles = {}
         cg_tiles = {}
@@ -118,35 +127,37 @@ def tile_spatialattentionlayer_pb_t_kernel(
         z_tiles = {}
         stats = {}
 
+        def pairs(b):
+            tiles = SIZES[b] // P
+            return [(r0, min(2, tiles - r0)) for r0 in range(0, tiles, 2)]
+
         def transpose_c(b):
-            for half in range(2):
+            for r0, n in pairs(b):
                 xt = ps_x.tile([P, BANK], F32)
-                for r2 in range(2):
-                    r = 2 * half + r2
-                    for u, src in enumerate((pq_tiles[b], att_tiles[b])):
+                for r2 in range(n):
+                    for u, src in enumerate((pq_all, att_all)):
                         col = (2 * r2 + u) * P
+                        first = STARTS[b] // P * P + (r0 + r2) * P
                         nc.tensor.transpose(
-                            xt[:, col : col + P],
-                            src[:].bitcast(F32)[:, r * P : (r + 1) * P],
-                            ident[:],
+                            xt[:, col : col + P], src[:].bitcast(F32)[:, first : first + P], ident[:]
                         )
-                xt_tiles[(b, half)] = xt
+                xt_tiles[(b, r0)] = xt
 
         def copy_c(b):
-            cg = work.tile([P, BLOCK * PACK], BF16, align_bytes=64)
+            cg = work.tile([P, SIZES[b] * PACK], BF16, align_bytes=64)
             cg_words = cg[:].bitcast(F32)
-            for half in range(2):
+            for r0, n in pairs(b):
                 nc.scalar.copy(
-                    out=cg_words[:, half * BANK : (half + 1) * BANK].rearrange(
-                        "q (r w u) -> q r w u", r=2, u=2
+                    out=cg_words[:, 2 * P * r0 : 2 * P * (r0 + n)].rearrange(
+                        "q (r w u) -> q r w u", r=n, u=2
                     ),
-                    in_=xt_tiles[(b, half)][:].rearrange("q (r u w) -> q r w u", r=2, u=2),
+                    in_=xt_tiles[(b, r0)][:, : 2 * P * n].rearrange("q (r u w) -> q r w u", r=n, u=2),
                 )
             cg_tiles[b] = cg
 
         def quantise_c(b):
-            c_codes = work.tile([P, BLOCK], U32, align_bytes=64)
-            c_scales = work.tile([P, BLOCK], U8, align_bytes=64)
+            c_codes = work.tile([P, SIZES[b]], U32, align_bytes=64)
+            c_scales = work.tile([P, SIZES[b]], U8, align_bytes=64)
             nc.vector.quantize_mx(
                 out=c_codes[:].bitcast(FP8X4), scales=c_scales[:], in_=cg_tiles[b][:]
             )
@@ -154,10 +165,13 @@ def tile_spatialattentionlayer_pb_t_kernel(
 
         def first_product(b):
             c_codes, c_scales = c_mx[b]
+            per_bank = BANK // SIZES[b]
             for t in range(PACK):
-                h_ps = ps_h.tile([P, BLOCK], F32)
+                if t % per_bank == 0:
+                    h_ps = ps_h.tile([P, BANK], F32)
+                spot = h_ps[:, (t % per_bank) * SIZES[b] : (t % per_bank + 1) * SIZES[b]]
                 nc.tensor.matmul_mx(
-                    out=h_ps[:],
+                    out=spot,
                     lhsT=w1_codes[:, t * P : (t + 1) * P].bitcast(FP8X4),
                     lhsT_scale=w1_scales[:, t * P : (t + 1) * P],
                     rhs=c_codes[:].bitcast(FP8X4),
@@ -165,37 +179,51 @@ def tile_spatialattentionlayer_pb_t_kernel(
                     start=True,
                     stop=True,
                 )
-                h_banks[(b, t)] = h_ps
+                h_banks[(b, t)] = spot
 
-        def relu_h(b):
-            h_plane = work.tile([P, PACK, BLOCK], BF16)
-            for t in range(PACK):
+        def relu_h(b, t0=0, t1=PACK):
+            if t0 == 0:
+                h_planes[b] = work.tile([P, PACK, SIZES[b]], BF16, name="h_plane")
+                hg_tiles[b] = work.tile([P, SIZES[b], PACK], BF16, align_bytes=64, name="hg", bufs=1)
+            h_plane = h_planes[b]
+            for t in range(t0, t1):
                 nc.scalar.activation(
                     out=h_plane[:, t, :],
-                    in_=h_banks[(b, t)][:],
+                    in_=h_banks[(b, t)],
                     func=ACT.Relu,
                     bias=b1[:, t : t + 1],
                     scale=1.0,
                 )
-            h_planes[b] = h_plane
 
-        def regroup_h_scalar(b):
-            hg = work.tile([P, BLOCK, PACK], BF16, align_bytes=64)
-            nc.scalar.copy(
-                out=hg[:, VECTOR_TOKENS:, :].rearrange("p (c i) t -> p c t i", i=4),
-                in_=h_planes[b][:, :, VECTOR_TOKENS:].rearrange("p t (c i) -> p c t i", i=4),
-            )
-            hg_tiles[b] = hg
+        def regroup_h(b, copy, first, last):
+            if first < last:
+                copy(
+                    out=hg_tiles[b][:, first:last, :].rearrange("p (c i) t -> p c t i", i=4),
+                    in_=h_planes[b][:, :, first:last].rearrange("p t (c i) -> p c t i", i=4),
+                )
 
-        def regroup_h_vector(b):
-            nc.vector.tensor_copy(
-                out=hg_tiles[b][:, :VECTOR_TOKENS, :].rearrange("p (c i) t -> p c t i", i=4),
-                in_=h_planes[b][:, :, :VECTOR_TOKENS].rearrange("p t (c i) -> p c t i", i=4),
-            )
+        def gp_share(b):
+            return GPSIMD_TOKENS
+
+        def regroup_gp(b):
+            first = SIZES[b] - scalar_share(b) - gp_share(b)
+            last = SIZES[b] - scalar_share(b)
+            if first < last:
+                nc.gpsimd.tensor_scalar(
+                    out=hg_tiles[b][:, first:last, :].rearrange("p (c i) t -> p c t i", i=4),
+                    in0=h_planes[b][:, :, first:last].rearrange("p t (c i) -> p c t i", i=4),
+                    scalar1=1.0,
+                    scalar2=0.0,
+                    op0=ALU.mult,
+                    op1=ALU.add,
+                )
+
+        def scalar_share(b):
+            return SCALAR_TOKENS[b]
 
         def quantise_h(b):
-            h_codes = work.tile([P, BLOCK], U32, align_bytes=64)
-            h_scales = work.tile([P, BLOCK], U8, align_bytes=64)
+            h_codes = work.tile([P, SIZES[b]], U32, align_bytes=64)
+            h_scales = work.tile([P, SIZES[b]], U8, align_bytes=64)
             nc.vector.quantize_mx(
                 out=h_codes[:].bitcast(FP8X4),
                 scales=h_scales[:],
@@ -205,10 +233,10 @@ def tile_spatialattentionlayer_pb_t_kernel(
 
         def second_product(b):
             h_codes, h_scales = h_mx[b]
-            for half in range(2):
+            for r0, n in pairs(b):
                 y_ps = ps_y.tile([P, 2, H], F32)
-                for r2 in range(2):
-                    r = 2 * half + r2
+                for r2 in range(n):
+                    r = r0 + r2
                     nc.tensor.matmul_mx(
                         out=y_ps[:, r2, :],
                         lhsT=h_codes[:, r * P : (r + 1) * P].bitcast(FP8X4),
@@ -218,15 +246,16 @@ def tile_spatialattentionlayer_pb_t_kernel(
                         start=True,
                         stop=True,
                     )
-                y_banks[(b, half)] = y_ps
+                    y_banks[(b, r)] = y_ps[:, r2, :]
 
         def add_bias(b):
-            z = work.tile([P, TILES, H], F32)
-            z_sum = work.tile([P, TILES], F32)
-            for r in range(TILES):
+            tiles = SIZES[b] // P
+            z = work.tile([P, tiles, H], F32)
+            z_sum = work.tile([P, tiles], F32)
+            for r in range(tiles):
                 nc.vector.scalar_tensor_tensor(
                     out=z[:, r, :],
-                    in0=y_banks[(b, r // 2)][:, r % 2, :],
+                    in0=y_banks[(b, r)],
                     scalar=1.0,
                     in1=b2_rows[:],
                     op0=ALU.mult,
@@ -237,14 +266,14 @@ def tile_spatialattentionlayer_pb_t_kernel(
             stats[(b, "z_sum")] = z_sum
 
         def mean(b):
-            neg_mean = work.tile([P, TILES], F32)
+            neg_mean = work.tile([P, SIZES[b] // P], F32)
             nc.scalar.mul(out=neg_mean[:], in_=stats[(b, "z_sum")][:], mul=-1.0 / H)
             stats[(b, "neg_mean")] = neg_mean
 
         def square_sums(b):
             neg_mean = stats[(b, "neg_mean")]
-            sq_sum = work.tile([P, TILES], F32)
-            for r in range(TILES):
+            sq_sum = work.tile([P, SIZES[b] // P], F32)
+            for r in range(SIZES[b] // P):
                 squares = work.tile([P, H], F32)
                 nc.scalar.activation(
                     out=squares[:],
@@ -257,7 +286,7 @@ def tile_spatialattentionlayer_pb_t_kernel(
             stats[(b, "sq_sum")] = sq_sum
 
         def inverse_deviation(b):
-            rstd = work.tile([P, TILES], F32)
+            rstd = work.tile([P, SIZES[b] // P], F32)
             nc.scalar.activation(
                 out=rstd[:],
                 in_=stats[(b, "sq_sum")][:],
@@ -270,8 +299,12 @@ def tile_spatialattentionlayer_pb_t_kernel(
         def normalise_and_store(b):
             neg_mean = stats[(b, "neg_mean")]
             rstd = stats[(b, "rstd")]
-            o = res.tile([P, TILES, H], F32)
-            for r in range(TILES):
+            tiles = SIZES[b] // P
+            o = res.tile([P, tiles, H], F32)
+            out_view = out_rows[STARTS[b] : STARTS[b] + SIZES[b], :].rearrange(
+                "(p r) h -> p r h", p=P
+            )
+            for r in range(tiles):
                 nc.vector.scalar_tensor_tensor(
                     out=o[:, r, :],
                     in0=z_tiles[b][:, r, :],
@@ -280,7 +313,7 @@ def tile_spatialattentionlayer_pb_t_kernel(
                     op0=ALU.add,
                     op1=ALU.mult,
                 )
-            for r in range(TILES):
+            for r in range(tiles):
                 nc.vector.scalar_tensor_tensor(
                     out=o[:, r, :],
                     in0=o[:, r, :],
@@ -289,36 +322,30 @@ def tile_spatialattentionlayer_pb_t_kernel(
                     op0=ALU.mult,
                     op1=ALU.add,
                 )
-                nc.sync.dma_start(out=out_blocks[b][:, r, :], in_=o[:, r, :])
+                nc.sync.dma_start(out=out_view[:, r, :], in_=o[:, r, :])
 
-        def in_range(b):
-            return 0 <= b < N_BLOCKS
+        def at(b, stage, *more):
+            if 0 <= b < N_BLOCKS:
+                stage(b, *more)
 
-        for i in range(-2, N_BLOCKS + 3):
-            if in_range(i + 2):
-                transpose_c(i + 2)
-            if in_range(i - 1):
-                regroup_h_vector(i - 1)
-            if in_range(i - 2):
-                add_bias(i - 2)
-            if in_range(i - 3):
-                square_sums(i - 3)
-            if in_range(i - 1):
-                quantise_h(i - 1)
-                second_product(i - 1)
-            if in_range(i + 1):
-                quantise_c(i + 1)
-            if in_range(i):
-                relu_h(i)
-            if in_range(i + 1):
-                first_product(i + 1)
-            if in_range(i - 3):
-                inverse_deviation(i - 3)
-            if in_range(i):
-                regroup_h_scalar(i)
-            if in_range(i - 2):
-                mean(i - 2)
-            if in_range(i + 2):
-                copy_c(i + 2)
-            if in_range(i - 3):
-                normalise_and_store(i - 3)
+        for k in range(-4, N_BLOCKS + 2):
+            at(k + 4, transpose_c)
+            at(k, quantise_h)
+            at(k - 1, add_bias)
+            at(k, second_product)
+            at(k + 1, regroup_gp)
+            at(k - 2, square_sums)
+            at(k + 1, lambda b: regroup_h(b, nc.vector.tensor_copy, 0, SIZES[b] - scalar_share(b) - gp_share(b)))
+            at(k + 3, quantise_c)
+            if k == -3:
+                nc.vector.tensor_copy(out=b1[:], in_=b1_bf[:])
+            at(k + 2, relu_h, 0, 2)
+            at(k - 2, inverse_deviation)
+            at(k + 2, relu_h, 2, 4)
+            at(k + 1, lambda b: regroup_h(b, nc.scalar.copy, SIZES[b] - scalar_share(b), SIZES[b]))
+            at(k + 3, first_product)
+            if k == -3:
+                prepare_w2()
+            at(k - 1, mean)
+            at(k + 4, copy_c)
+            at(k - 2, normalise_and_store)

@@ -23,8 +23,7 @@ BLOCK = 512
 N_BLOCKS = TOKENS // BLOCK
 SIZES = (BLOCK,) * N_BLOCKS
 STARTS = tuple(BLOCK * b for b in range(N_BLOCKS))
-GPSIMD_TOKENS = 192
-SCALAR_TOKENS = (0,) * 5 + (64,) * (N_BLOCKS - 8) + (320,) * 3
+VECTOR_REGROUPS = 2
 
 FLOPS = 2 * TOKENS * C * F + 2 * TOKENS * F * H
 
@@ -42,7 +41,8 @@ def tile_spatialattentionlayer_pb_t_kernel(
         work = ctx.enter_context(tc.tile_pool(name="work", bufs=4))
         res = ctx.enter_context(tc.tile_pool(name="res", bufs=3))
         ps_x = ctx.enter_context(tc.psum_pool(name="ps_x", bufs=2))
-        ps_h = ctx.enter_context(tc.psum_pool(name="ps_h", bufs=4))
+        ps_h = ctx.enter_context(tc.psum_pool(name="ps_h", bufs=3))
+        ps_c = ctx.enter_context(tc.psum_pool(name="ps_c", bufs=1))
         ps_y = ctx.enter_context(tc.psum_pool(name="ps_y", bufs=2))
         ctx.enter_context(tc.manual_schedule())
 
@@ -84,6 +84,8 @@ def tile_spatialattentionlayer_pb_t_kernel(
 
         ident = const.tile([P, P], F32)
         make_identity(nc, ident[:])
+        ident_bf = const.tile([P, P], BF16)
+        make_identity(nc, ident_bf[:])
         eps = const.tile([P, 1], F32)
         nc.vector.memset(eps[:], LN_EPS)
         first_use = const.tile([P, 1], F32)
@@ -107,6 +109,12 @@ def tile_spatialattentionlayer_pb_t_kernel(
         w2_grouped = const.tile([P, H, PACK], BF16, align_bytes=64)
         w2_codes = const.tile([P, H], U32, align_bytes=64)
         w2_scales = const.tile([P, H], U8, align_bytes=64)
+
+        affine = ps_c.tile([P, 2, H], F32)
+
+        def prepare_affine():
+            for a, rows in enumerate((g_rows, b_rows)):
+                nc.tensor.matmul(affine[:, a, :], lhsT=ident_bf[:], rhs=rows[:], start=True, stop=True)
 
         def prepare_w2():
             nc.vector.tensor_copy(out=w2_grouped[:], in_=w2_raw[:].rearrange("p t j -> p j t"))
@@ -195,31 +203,23 @@ def tile_spatialattentionlayer_pb_t_kernel(
                     scale=1.0,
                 )
 
-        def regroup_h(b, copy, first, last):
-            if first < last:
-                copy(
-                    out=hg_tiles[b][:, first:last, :].rearrange("p (c i) t -> p c t i", i=4),
-                    in_=h_planes[b][:, :, first:last].rearrange("p t (c i) -> p c t i", i=4),
-                )
-
-        def gp_share(b):
-            return GPSIMD_TOKENS
-
-        def regroup_gp(b):
-            first = SIZES[b] - scalar_share(b) - gp_share(b)
-            last = SIZES[b] - scalar_share(b)
-            if first < last:
+        def regroup_on_gpsimd(b):
+            if b >= VECTOR_REGROUPS:
                 nc.gpsimd.tensor_scalar(
-                    out=hg_tiles[b][:, first:last, :].rearrange("p (c i) t -> p c t i", i=4),
-                    in0=h_planes[b][:, :, first:last].rearrange("p t (c i) -> p c t i", i=4),
+                    out=hg_tiles[b][:].rearrange("p (c i) t -> p c t i", i=4),
+                    in0=h_planes[b][:].rearrange("p t (c i) -> p c t i", i=4),
                     scalar1=1.0,
                     scalar2=0.0,
                     op0=ALU.mult,
                     op1=ALU.add,
                 )
 
-        def scalar_share(b):
-            return SCALAR_TOKENS[b]
+        def regroup_on_vector(b):
+            if b < VECTOR_REGROUPS:
+                nc.vector.tensor_copy(
+                    out=hg_tiles[b][:].rearrange("p (c i) t -> p c t i", i=4),
+                    in_=h_planes[b][:].rearrange("p t (c i) -> p c t i", i=4),
+                )
 
         def quantise_h(b):
             h_codes = work.tile([P, SIZES[b]], U32, align_bytes=64)
@@ -309,7 +309,7 @@ def tile_spatialattentionlayer_pb_t_kernel(
                     out=o[:, r, :],
                     in0=z_tiles[b][:, r, :],
                     scalar=neg_mean[:, r : r + 1],
-                    in1=g_rows[:],
+                    in1=affine[:, 0, :],
                     op0=ALU.add,
                     op1=ALU.mult,
                 )
@@ -318,7 +318,7 @@ def tile_spatialattentionlayer_pb_t_kernel(
                     out=o[:, r, :],
                     in0=o[:, r, :],
                     scalar=rstd[:, r : r + 1],
-                    in1=b_rows[:],
+                    in1=affine[:, 1, :],
                     op0=ALU.mult,
                     op1=ALU.add,
                 )
@@ -330,22 +330,23 @@ def tile_spatialattentionlayer_pb_t_kernel(
 
         for k in range(-4, N_BLOCKS + 2):
             at(k + 4, transpose_c)
+            at(k + 3, quantise_c)
             at(k, quantise_h)
             at(k - 1, add_bias)
             at(k, second_product)
-            at(k + 1, regroup_gp)
+            at(k + 1, regroup_on_gpsimd)
             at(k - 2, square_sums)
-            at(k + 1, lambda b: regroup_h(b, nc.vector.tensor_copy, 0, SIZES[b] - scalar_share(b) - gp_share(b)))
-            at(k + 3, quantise_c)
+            at(k + 1, regroup_on_vector)
             if k == -3:
                 nc.vector.tensor_copy(out=b1[:], in_=b1_bf[:])
             at(k + 2, relu_h, 0, 2)
             at(k - 2, inverse_deviation)
             at(k + 2, relu_h, 2, 4)
-            at(k + 1, lambda b: regroup_h(b, nc.scalar.copy, SIZES[b] - scalar_share(b), SIZES[b]))
             at(k + 3, first_product)
             if k == -3:
                 prepare_w2()
+            if k == -1:
+                prepare_affine()
             at(k - 1, mean)
             at(k + 4, copy_c)
             at(k - 2, normalise_and_store)

@@ -23,7 +23,9 @@ BLOCK = 512
 N_BLOCKS = TOKENS // BLOCK
 SIZES = (BLOCK,) * N_BLOCKS
 STARTS = tuple(BLOCK * b for b in range(N_BLOCKS))
+VECTOR_RELUS = {0: (1, 2, 3), 1: (3,), 2: (3,)}
 VECTOR_REGROUPS = 2
+H_BANKS = 3
 
 FLOPS = 2 * TOKENS * C * F + 2 * TOKENS * F * H
 
@@ -41,7 +43,7 @@ def tile_spatialattentionlayer_pb_t_kernel(
         work = ctx.enter_context(tc.tile_pool(name="work", bufs=4))
         res = ctx.enter_context(tc.tile_pool(name="res", bufs=3))
         ps_x = ctx.enter_context(tc.psum_pool(name="ps_x", bufs=2))
-        ps_h = ctx.enter_context(tc.psum_pool(name="ps_h", bufs=3))
+        ps_h = ctx.enter_context(tc.psum_pool(name="ps_h", bufs=H_BANKS))
         ps_c = ctx.enter_context(tc.psum_pool(name="ps_c", bufs=1))
         ps_y = ctx.enter_context(tc.psum_pool(name="ps_y", bufs=2))
         ctx.enter_context(tc.manual_schedule())
@@ -155,7 +157,8 @@ def tile_spatialattentionlayer_pb_t_kernel(
             cg = work.tile([P, SIZES[b] * PACK], BF16, align_bytes=64)
             cg_words = cg[:].bitcast(F32)
             for r0, n in pairs(b):
-                nc.scalar.copy(
+                copy = nc.vector.tensor_copy if (b, r0) == (0, 2) else nc.scalar.copy
+                copy(
                     out=cg_words[:, 2 * P * r0 : 2 * P * (r0 + n)].rearrange(
                         "q (r w u) -> q r w u", r=n, u=2
                     ),
@@ -171,13 +174,20 @@ def tile_spatialattentionlayer_pb_t_kernel(
             )
             c_mx[b] = (c_codes, c_scales)
 
-        def first_product(b):
-            c_codes, c_scales = c_mx[b]
+        slots = []
+        for b in range(N_BLOCKS):
             per_bank = BANK // SIZES[b]
-            for t in range(PACK):
-                if t % per_bank == 0:
-                    h_ps = ps_h.tile([P, BANK], F32)
-                spot = h_ps[:, (t % per_bank) * SIZES[b] : (t % per_bank + 1) * SIZES[b]]
+            for t in range(0, PACK, per_bank):
+                slots.append((b, range(t, t + per_bank)))
+        filled = [0]
+
+        def fill_bank():
+            b, chunks = slots[filled[0]]
+            filled[0] += 1
+            c_codes, c_scales = c_mx[b]
+            h_ps = ps_h.tile([P, BANK], F32)
+            for n, t in enumerate(chunks):
+                spot = h_ps[:, n * SIZES[b] : (n + 1) * SIZES[b]]
                 nc.tensor.matmul_mx(
                     out=spot,
                     lhsT=w1_codes[:, t * P : (t + 1) * P].bitcast(FP8X4),
@@ -189,21 +199,33 @@ def tile_spatialattentionlayer_pb_t_kernel(
                 )
                 h_banks[(b, t)] = spot
 
-        def relu_h(b, t0=0, t1=PACK):
-            if t0 == 0:
+        def relu_h(b, s):
+            per_bank = BANK // SIZES[b]
+            if s == 0:
                 h_planes[b] = work.tile([P, PACK, SIZES[b]], BF16, name="h_plane")
-                hg_tiles[b] = work.tile([P, SIZES[b], PACK], BF16, align_bytes=64, name="hg", bufs=1)
-            h_plane = h_planes[b]
-            for t in range(t0, t1):
-                nc.scalar.activation(
-                    out=h_plane[:, t, :],
-                    in_=h_banks[(b, t)],
-                    func=ACT.Relu,
-                    bias=b1[:, t : t + 1],
-                    scale=1.0,
-                )
+            for t in range(s * per_bank, (s + 1) * per_bank):
+                if t in VECTOR_RELUS.get(b, ()):
+                    nc.vector.tensor_scalar(out=h_planes[b][:, t, :], in0=h_banks[(b, t)], scalar1=b1[:, t : t + 1], scalar2=0.0, op0=ALU.add, op1=ALU.max)
+                else:
+                    nc.scalar.activation(
+                        out=h_planes[b][:, t, :],
+                        in_=h_banks[(b, t)],
+                        func=ACT.Relu,
+                        bias=b1[:, t : t + 1],
+                        scale=1.0,
+                    )
+            if filled[0] < len(slots) and slots[filled[0]][0] in c_mx:
+                fill_bank()
+
+        def first_banks(b):
+            while filled[0] < H_BANKS and slots[filled[0]][0] <= b:
+                fill_bank()
+
+        def new_hg(b):
+            hg_tiles[b] = work.tile([P, SIZES[b], PACK], BF16, align_bytes=64, name="hg", bufs=1)
 
         def regroup_on_gpsimd(b):
+            new_hg(b)
             if b >= VECTOR_REGROUPS:
                 nc.gpsimd.tensor_scalar(
                     out=hg_tiles[b][:].rearrange("p (c i) t -> p c t i", i=4),
@@ -328,23 +350,27 @@ def tile_spatialattentionlayer_pb_t_kernel(
             if 0 <= b < N_BLOCKS:
                 stage(b, *more)
 
+        def relu_banks(b, first, last):
+            for s in range(first, last):
+                relu_h(b, s)
+
         for k in range(-4, N_BLOCKS + 2):
             at(k + 4, transpose_c)
             at(k + 3, quantise_c)
             at(k, quantise_h)
             at(k - 1, add_bias)
-            at(k, second_product)
             at(k + 1, regroup_on_gpsimd)
             at(k - 2, square_sums)
             at(k + 1, regroup_on_vector)
             if k == -3:
                 nc.vector.tensor_copy(out=b1[:], in_=b1_bf[:])
-            at(k + 2, relu_h, 0, 2)
+            at(k + 3, first_banks)
+            at(k + 2, relu_banks, 0, 2)
             at(k - 2, inverse_deviation)
-            at(k + 2, relu_h, 2, 4)
-            at(k + 3, first_product)
             if k == -3:
                 prepare_w2()
+            at(k, second_product)
+            at(k + 2, relu_banks, 2, 4)
             if k == -1:
                 prepare_affine()
             at(k - 1, mean)

@@ -75,19 +75,17 @@ def tile_spatialattentionlayer_pb_t_kernel(
         nc.sync.dma_start(out=w2_raw[:], in_=Wf2.rearrange("(p t) j -> p t j", t=PACK))
         load_block(2)
         load_block(3)
-        b2_rows = const.tile([P, H], BF16)
-        nc.sync.dma_start(out=b2_rows[:], in_=bf2.partition_broadcast(P))
-        g_rows = const.tile([P, H], BF16)
-        nc.sync.dma_start(out=g_rows[:], in_=ln_g.partition_broadcast(P))
-        b_rows = const.tile([P, H], BF16)
-        nc.sync.dma_start(out=b_rows[:], in_=ln_b.partition_broadcast(P))
+        vectors = const.tile([P, 3, H], BF16)
+        nc.gpsimd.memset(vectors[:], 0.0)
+        for v, vec in enumerate((bf2, ln_g, ln_b)):
+            nc.sync.dma_start(out=vectors[0:1, v, :], in_=vec.rearrange("(o h) -> o h", o=1))
         for b in range(4, N_BLOCKS):
             load_block(b)
 
         ident = const.tile([P, P], F32)
         make_identity(nc, ident[:])
-        ident_bf = const.tile([P, P], BF16)
-        make_identity(nc, ident_bf[:])
+        ones = const.tile([P, P], BF16)
+        nc.gpsimd.memset(ones[:], 1.0)
         eps = const.tile([P, 1], F32)
         nc.vector.memset(eps[:], LN_EPS)
         first_use = const.tile([P, 1], F32)
@@ -113,10 +111,13 @@ def tile_spatialattentionlayer_pb_t_kernel(
         w2_scales = const.tile([P, H], U8, align_bytes=64)
 
         affine = ps_c.tile([P, 2, H], F32)
+        b2_rows = const.tile([P, H], F32)
 
-        def prepare_affine():
-            for a, rows in enumerate((g_rows, b_rows)):
-                nc.tensor.matmul(affine[:, a, :], lhsT=ident_bf[:], rhs=rows[:], start=True, stop=True)
+        def prepare_vectors():
+            y_ps = ps_y.tile([P, 2, H], F32)
+            for v, rows in enumerate((y_ps[:, 0, :], affine[:, 0, :], affine[:, 1, :])):
+                nc.tensor.matmul(rows, lhsT=ones[:], rhs=vectors[:, v, :], start=True, stop=True)
+            nc.vector.tensor_copy(out=b2_rows[:], in_=y_ps[:, 0, :])
 
         def prepare_w2():
             nc.vector.tensor_copy(out=w2_grouped[:], in_=w2_raw[:].rearrange("p t j -> p j t"))
@@ -369,10 +370,10 @@ def tile_spatialattentionlayer_pb_t_kernel(
             at(k - 2, inverse_deviation)
             if k == -3:
                 prepare_w2()
+            if k == -1:
+                prepare_vectors()
             at(k, second_product)
             at(k + 2, relu_banks, 2, 4)
-            if k == -1:
-                prepare_affine()
             at(k - 1, mean)
             at(k + 4, copy_c)
             at(k - 2, normalise_and_store)

@@ -229,8 +229,8 @@ def tile_spatialattentionlayer_pb_t_kernel(
             new_hg(b)
             if b >= VECTOR_REGROUPS:
                 nc.gpsimd.tensor_scalar(
-                    out=hg_tiles[b][:].rearrange("p (c i) t -> p c t i", i=4),
-                    in0=h_planes[b][:].rearrange("p t (c i) -> p c t i", i=4),
+                    out=hg_tiles[b][:],
+                    in0=h_planes[b][:].rearrange("p t n -> p n t"),
                     scalar1=1.0,
                     scalar2=0.0,
                     op0=ALU.mult,

@@ -23,8 +23,8 @@ BLOCK = 512
 N_BLOCKS = TOKENS // BLOCK
 SIZES = (BLOCK,) * N_BLOCKS
 STARTS = tuple(BLOCK * b for b in range(N_BLOCKS))
-VECTOR_RELUS = {0: (1, 2, 3), 1: (3,), 2: (3,)}
-VECTOR_REGROUPS = 2
+VECTOR_RELUS = {0: (1, 2, 3), 1: (3,)}
+VECTOR_REGROUPS = {0: 256, 1: 256}
 H_BANKS = 3
 
 FLOPS = 2 * TOKENS * C * F + 2 * TOKENS * F * H
@@ -41,7 +41,7 @@ def tile_spatialattentionlayer_pb_t_kernel(
     with ExitStack() as ctx:
         const = ctx.enter_context(tc.tile_pool(name="const", bufs=1))
         work = ctx.enter_context(tc.tile_pool(name="work", bufs=4))
-        res = ctx.enter_context(tc.tile_pool(name="res", bufs=3))
+        res = ctx.enter_context(tc.tile_pool(name="res", bufs=N_BLOCKS))
         ps_x = ctx.enter_context(tc.psum_pool(name="ps_x", bufs=2))
         ps_h = ctx.enter_context(tc.psum_pool(name="ps_h", bufs=H_BANKS))
         ps_c = ctx.enter_context(tc.psum_pool(name="ps_c", bufs=1))
@@ -227,21 +227,22 @@ def tile_spatialattentionlayer_pb_t_kernel(
 
         def regroup_on_gpsimd(b):
             new_hg(b)
-            if b >= VECTOR_REGROUPS:
-                nc.gpsimd.tensor_scalar(
-                    out=hg_tiles[b][:],
-                    in0=h_planes[b][:].rearrange("p t n -> p n t"),
-                    scalar1=1.0,
-                    scalar2=0.0,
-                    op0=ALU.mult,
-                    op1=ALU.add,
-                )
+            first = VECTOR_REGROUPS.get(b, 0)
+            nc.gpsimd.tensor_scalar(
+                out=hg_tiles[b][:, first:, :],
+                in0=h_planes[b][:, :, first:].rearrange("p t n -> p n t"),
+                scalar1=1.0,
+                scalar2=0.0,
+                op0=ALU.mult,
+                op1=ALU.add,
+            )
 
         def regroup_on_vector(b):
-            if b < VECTOR_REGROUPS:
+            last = VECTOR_REGROUPS.get(b, 0)
+            if last > 0:
                 nc.vector.tensor_copy(
-                    out=hg_tiles[b][:].rearrange("p (c i) t -> p c t i", i=4),
-                    in_=h_planes[b][:].rearrange("p t (c i) -> p c t i", i=4),
+                    out=hg_tiles[b][:, :last, :].rearrange("p (c i) t -> p c t i", i=4),
+                    in_=h_planes[b][:, :, :last].rearrange("p t (c i) -> p c t i", i=4),
                 )
 
         def quantise_h(b):
@@ -319,14 +320,12 @@ def tile_spatialattentionlayer_pb_t_kernel(
             )
             stats[(b, "rstd")] = rstd
 
-        def normalise_and_store(b):
+        o_tiles = {}
+
+        def centre_and_scale(b):
             neg_mean = stats[(b, "neg_mean")]
-            rstd = stats[(b, "rstd")]
             tiles = SIZES[b] // P
             o = res.tile([P, tiles, H], F32)
-            out_view = out_rows[STARTS[b] : STARTS[b] + SIZES[b], :].rearrange(
-                "(p r) h -> p r h", p=P
-            )
             for r in range(tiles):
                 nc.vector.scalar_tensor_tensor(
                     out=o[:, r, :],
@@ -336,6 +335,15 @@ def tile_spatialattentionlayer_pb_t_kernel(
                     op0=ALU.add,
                     op1=ALU.mult,
                 )
+            o_tiles[b] = o
+
+        def normalise_and_store(b):
+            rstd = stats[(b, "rstd")]
+            tiles = SIZES[b] // P
+            o = o_tiles[b]
+            out_view = out_rows[STARTS[b] : STARTS[b] + SIZES[b], :].rearrange(
+                "(p r) h -> p r h", p=P
+            )
             for r in range(tiles):
                 nc.vector.scalar_tensor_tensor(
                     out=o[:, r, :],
@@ -351,29 +359,28 @@ def tile_spatialattentionlayer_pb_t_kernel(
             if 0 <= b < N_BLOCKS:
                 stage(b, *more)
 
-        def relu_banks(b, first, last):
-            for s in range(first, last):
-                relu_h(b, s)
-
-        for k in range(-4, N_BLOCKS + 2):
+        for k in range(-4, N_BLOCKS + 1):
             at(k + 4, transpose_c)
             at(k + 3, quantise_c)
             at(k, quantise_h)
-            at(k - 1, add_bias)
             at(k + 1, regroup_on_gpsimd)
-            at(k - 2, square_sums)
             at(k + 1, regroup_on_vector)
             if k == -3:
                 nc.vector.tensor_copy(out=b1[:], in_=b1_bf[:])
             at(k + 3, first_banks)
-            at(k + 2, relu_banks, 0, 2)
-            at(k - 2, inverse_deviation)
+            at(k - 1, centre_and_scale)
+            at(k + 2, relu_h, 0)
+            at(k, second_product)
+            at(k, add_bias)
+            at(k + 2, relu_h, 1)
+            at(k - 1, square_sums)
             if k == -3:
                 prepare_w2()
-            if k == -1:
+            at(k + 2, relu_h, 2)
+            at(k - 1, inverse_deviation)
+            at(k + 2, relu_h, 3)
+            if k == -2:
                 prepare_vectors()
-            at(k, second_product)
-            at(k + 2, relu_banks, 2, 4)
-            at(k - 1, mean)
             at(k + 4, copy_c)
-            at(k - 2, normalise_and_store)
+            at(k, mean)
+            at(k - 1, normalise_and_store)

from contextlib import ExitStack

import concourse.mybir as mybir
from concourse.masks import make_identity

F32 = mybir.dt.float32
BF16 = mybir.dt.bfloat16
U32 = mybir.dt.uint32
U8 = mybir.dt.uint8
FP8X4 = mybir.dt.float8_e4m3fn_x4
ALU = mybir.AluOpType
ACT = mybir.ActivationFunctionType

P = 128
PACK = 4
TOKENS = 4 * 2048
H = 256
C = 2 * H
F = 512
BANK = 512
LN_EPS = 1e-5
BLOCK = 512
N_BLOCKS = TOKENS // BLOCK
SIZES = (BLOCK,) * N_BLOCKS
STARTS = tuple(BLOCK * b for b in range(N_BLOCKS))
VECTOR_RELUS = {0: (1, 2, 3), 1: (3,)}
VECTOR_REGROUPS = {0: 256, 1: 256}
H_BANKS = 3

FLOPS = 2 * TOKENS * C * F + 2 * TOKENS * F * H


def tile_spatialattentionlayer_pb_t_kernel(
    tc, pq, attended, Wf1, bf1, Wf2, bf2, ln_g, ln_b, out
):
    nc = tc.nc
    pq_rows = pq.rearrange("b n h -> (b n) h")
    att_rows = attended.rearrange("b n h -> (b n) h")
    out_rows = out.rearrange("b n h -> (b n) h")

    with ExitStack() as ctx:
        const = ctx.enter_context(tc.tile_pool(name="const", bufs=1))
        work = ctx.enter_context(tc.tile_pool(name="work", bufs=4))
        res = ctx.enter_context(tc.tile_pool(name="res", bufs=N_BLOCKS))
        ps_x = ctx.enter_context(tc.psum_pool(name="ps_x", bufs=2))
        ps_h = ctx.enter_context(tc.psum_pool(name="ps_h", bufs=H_BANKS))
        ps_c = ctx.enter_context(tc.psum_pool(name="ps_c", bufs=1))
        ps_y = ctx.enter_context(tc.psum_pool(name="ps_y", bufs=2))
        ctx.enter_context(tc.manual_schedule())

        pq_all = const.tile([P, TOKENS // P * H], BF16)
        att_all = const.tile([P, TOKENS // P * H], BF16)

        def columns(b):
            return slice(STARTS[b] // P * H, (STARTS[b] + SIZES[b]) // P * H)

        def load_block(b):
            rows = slice(STARTS[b], STARTS[b] + SIZES[b])
            for sb, hbm in ((pq_all, pq_rows), (att_all, att_rows)):
                nc.sync.dma_start(
                    out=sb[:, columns(b)], in_=hbm[rows, :].rearrange("(p r) h -> p (r h)", p=P)
                )

        w1_raw = const.tile([P, PACK, F], BF16)
        for u in range(2):
            nc.sync.dma_start(
                out=w1_raw[:, 2 * u : 2 * u + 2, :],
                in_=Wf1[H * u : H * (u + 1), :].rearrange("(q e) f -> q e f", e=2),
            )
        load_block(0)
        load_block(1)
        b1_bf = const.tile([P, PACK], BF16)
        nc.sync.dma_start(out=b1_bf[:], in_=bf1.rearrange("(p t) -> p t", t=PACK))
        w2_raw = const.tile([P, PACK, H], BF16)
        nc.sync.dma_start(out=w2_raw[:], in_=Wf2.rearrange("(p t) j -> p t j", t=PACK))
        load_block(2)
        load_block(3)
        vectors = const.tile([P, 3, H], BF16)
        nc.gpsimd.memset(vectors[:], 0.0)
        for v, vec in enumerate((bf2, ln_g, ln_b)):
            nc.sync.dma_start(out=vectors[0:1, v, :], in_=vec.rearrange("(o h) -> o h", o=1))
        for b in range(4, N_BLOCKS):
            load_block(b)

        ident = const.tile([P, P], F32)
        make_identity(nc, ident[:])
        ones = const.tile([P, P], BF16)
        nc.gpsimd.memset(ones[:], 1.0)
        eps = const.tile([P, 1], F32)
        nc.vector.memset(eps[:], LN_EPS)
        first_use = const.tile([P, 1], F32)
        nc.scalar.activation(
            out=first_use[:], in_=eps[:], func=ACT.Abs_reciprocal_sqrt, bias=eps[:, 0:1], scale=1.0
        )

        w1_grouped = const.tile([P, F, PACK], BF16, align_bytes=64)
        nc.vector.tensor_copy(
            out=w1_grouped[:].rearrange("q (t m) s -> q t m s", t=PACK),
            in_=w1_raw[:].rearrange("q s (m t) -> q t m s", t=PACK),
        )
        w1_codes = const.tile([P, F], U32, align_bytes=64)
        w1_scales = const.tile([P, F], U8, align_bytes=64)
        nc.vector.quantize_mx(
            out=w1_codes[:].bitcast(FP8X4),
            scales=w1_scales[:],
            in_=w1_grouped[:].rearrange("q f s -> q (f s)"),
        )
        b1 = const.tile([P, PACK], F32)
        w2_grouped = const.tile([P, H, PACK], BF16, align_bytes=64)
        w2_codes = const.tile([P, H], U32, align_bytes=64)
        w2_scales = const.tile([P, H], U8, align_bytes=64)

        affine = ps_c.tile([P, 2, H], F32)
        b2_rows = const.tile([P, H], F32)

        def prepare_vectors():
            y_ps = ps_y.tile([P, 2, H], F32)
            for v, rows in enumerate((y_ps[:, 0, :], affine[:, 0, :], affine[:, 1, :])):
                nc.tensor.matmul(rows, lhsT=ones[:], rhs=vectors[:, v, :], start=True, stop=True)
            nc.vector.tensor_copy(out=b2_rows[:], in_=y_ps[:, 0, :])

        def prepare_w2():
            nc.vector.tensor_copy(out=w2_grouped[:], in_=w2_raw[:].rearrange("p t j -> p j t"))
            nc.vector.quantize_mx(
                out=w2_codes[:].bitcast(FP8X4),
                scales=w2_scales[:],
                in_=w2_grouped[:].rearrange("p j t -> p (j t)"),
            )

        xt_tiles = {}
        cg_tiles = {}
        c_mx = {}
        h_banks = {}
        h_planes = {}
        hg_tiles = {}
        h_mx = {}
        y_banks = {}
        z_tiles = {}
        stats = {}

        def pairs(b):
            tiles = SIZES[b] // P
            return [(r0, min(2, tiles - r0)) for r0 in range(0, tiles, 2)]

        def transpose_c(b):
            for r0, n in pairs(b):
                xt = ps_x.tile([P, BANK], F32)
                for r2 in range(n):
                    for u, src in enumerate((pq_all, att_all)):
                        col = (2 * r2 + u) * P
                        first = STARTS[b] // P * P + (r0 + r2) * P
                        nc.tensor.transpose(
                            xt[:, col : col + P], src[:].bitcast(F32)[:, first : first + P], ident[:]
                        )
                xt_tiles[(b, r0)] = xt

        def copy_c(b):
            cg = work.tile([P, SIZES[b] * PACK], BF16, align_bytes=64)
            cg_words = cg[:].bitcast(F32)
            for r0, n in pairs(b):
                copy = nc.vector.tensor_copy if (b, r0) == (0, 2) else nc.scalar.copy
                copy(
                    out=cg_words[:, 2 * P * r0 : 2 * P * (r0 + n)].rearrange(
                        "q (r w u) -> q r w u", r=n, u=2
                    ),
                    in_=xt_tiles[(b, r0)][:, : 2 * P * n].rearrange("q (r u w) -> q r w u", r=n, u=2),
                )
            cg_tiles[b] = cg

        def quantise_c(b):
            c_codes = work.tile([P, SIZES[b]], U32, align_bytes=64)
            c_scales = work.tile([P, SIZES[b]], U8, align_bytes=64)
            nc.vector.quantize_mx(
                out=c_codes[:].bitcast(FP8X4), scales=c_scales[:], in_=cg_tiles[b][:]
            )
            c_mx[b] = (c_codes, c_scales)

        slots = []
        for b in range(N_BLOCKS):
            per_bank = BANK // SIZES[b]
            for t in range(0, PACK, per_bank):
                slots.append((b, range(t, t + per_bank)))
        filled = [0]

        def fill_bank():
            b, chunks = slots[filled[0]]
            filled[0] += 1
            c_codes, c_scales = c_mx[b]
            h_ps = ps_h.tile([P, BANK], F32)
            for n, t in enumerate(chunks):
                spot = h_ps[:, n * SIZES[b] : (n + 1) * SIZES[b]]
                nc.tensor.matmul_mx(
                    out=spot,
                    lhsT=w1_codes[:, t * P : (t + 1) * P].bitcast(FP8X4),
                    lhsT_scale=w1_scales[:, t * P : (t + 1) * P],
                    rhs=c_codes[:].bitcast(FP8X4),
                    rhs_scale=c_scales[:],
                    start=True,
                    stop=True,
                )
                h_banks[(b, t)] = spot

        def relu_h(b, s):
            per_bank = BANK // SIZES[b]
            if s == 0:
                h_planes[b] = work.tile([P, PACK, SIZES[b]], BF16, name="h_plane")
            for t in range(s * per_bank, (s + 1) * per_bank):
                if t in VECTOR_RELUS.get(b, ()):
                    nc.vector.tensor_scalar(out=h_planes[b][:, t, :], in0=h_banks[(b, t)], scalar1=b1[:, t : t + 1], scalar2=0.0, op0=ALU.add, op1=ALU.max)
                else:
                    nc.scalar.activation(
                        out=h_planes[b][:, t, :],
                        in_=h_banks[(b, t)],
                        func=ACT.Relu,
                        bias=b1[:, t : t + 1],
                        scale=1.0,
                    )
            if filled[0] < len(slots) and slots[filled[0]][0] in c_mx:
                fill_bank()

        def first_banks(b):
            while filled[0] < H_BANKS and slots[filled[0]][0] <= b:
                fill_bank()

        def new_hg(b):
            hg_tiles[b] = work.tile([P, SIZES[b], PACK], BF16, align_bytes=64, name="hg", bufs=1)

        def regroup_on_gpsimd(b):
            new_hg(b)
            first = VECTOR_REGROUPS.get(b, 0)
            nc.gpsimd.tensor_scalar(
                out=hg_tiles[b][:, first:, :],
                in0=h_planes[b][:, :, first:].rearrange("p t n -> p n t"),
                scalar1=1.0,
                scalar2=0.0,
                op0=ALU.mult,
                op1=ALU.add,
            )

        def regroup_on_vector(b):
            last = VECTOR_REGROUPS.get(b, 0)
            if last > 0:
                nc.vector.tensor_copy(
                    out=hg_tiles[b][:, :last, :].rearrange("p (c i) t -> p c t i", i=4),
                    in_=h_planes[b][:, :, :last].rearrange("p t (c i) -> p c t i", i=4),
                )

        def quantise_h(b):
            h_codes = work.tile([P, SIZES[b]], U32, align_bytes=64)
            h_scales = work.tile([P, SIZES[b]], U8, align_bytes=64)
            nc.vector.quantize_mx(
                out=h_codes[:].bitcast(FP8X4),
                scales=h_scales[:],
                in_=hg_tiles[b][:].rearrange("p n t -> p (n t)"),
            )
            h_mx[b] = (h_codes, h_scales)

        def second_product(b):
            h_codes, h_scales = h_mx[b]
            for r0, n in pairs(b):
                y_ps = ps_y.tile([P, 2, H], F32)
                for r2 in range(n):
                    r = r0 + r2
                    nc.tensor.matmul_mx(
                        out=y_ps[:, r2, :],
                        lhsT=h_codes[:, r * P : (r + 1) * P].bitcast(FP8X4),
                        lhsT_scale=h_scales[:, r * P : (r + 1) * P],
                        rhs=w2_codes[:].bitcast(FP8X4),
                        rhs_scale=w2_scales[:],
                        start=True,
                        stop=True,
                    )
                    y_banks[(b, r)] = y_ps[:, r2, :]

        def add_bias(b):
            tiles = SIZES[b] // P
            z = work.tile([P, tiles, H], F32)
            z_sum = work.tile([P, tiles], F32)
            for r in range(tiles):
                nc.vector.scalar_tensor_tensor(
                    out=z[:, r, :],
                    in0=y_banks[(b, r)],
                    scalar=1.0,
                    in1=b2_rows[:],
                    op0=ALU.mult,
                    op1=ALU.add,
                    accum_out=z_sum[:, r : r + 1],
                )
            z_tiles[b] = z
            stats[(b, "z_sum")] = z_sum

        def mean(b):
            neg_mean = work.tile([P, SIZES[b] // P], F32)
            nc.scalar.mul(out=neg_mean[:], in_=stats[(b, "z_sum")][:], mul=-1.0 / H)
            stats[(b, "neg_mean")] = neg_mean

        def square_sums(b):
            neg_mean = stats[(b, "neg_mean")]
            sq_sum = work.tile([P, SIZES[b] // P], F32)
            for r in range(SIZES[b] // P):
                squares = work.tile([P, H], F32)
                nc.scalar.activation(
                    out=squares[:],
                    in_=z_tiles[b][:, r, :],
                    func=ACT.Square,
                    bias=neg_mean[:, r : r + 1],
                    scale=1.0,
                    accum_out=sq_sum[:, r : r + 1],
                )
            stats[(b, "sq_sum")] = sq_sum

        def inverse_deviation(b):
            rstd = work.tile([P, SIZES[b] // P], F32)
            nc.scalar.activation(
                out=rstd[:],
                in_=stats[(b, "sq_sum")][:],
                func=ACT.Abs_reciprocal_sqrt,
                bias=eps[:, 0:1],
                scale=1.0 / H,
            )
            stats[(b, "rstd")] = rstd

        o_tiles = {}

        def centre_and_scale(b):
            neg_mean = stats[(b, "neg_mean")]
            tiles = SIZES[b] // P
            o = res.tile([P, tiles, H], F32)
            for r in range(tiles):
                nc.vector.scalar_tensor_tensor(
                    out=o[:, r, :],
                    in0=z_tiles[b][:, r, :],
                    scalar=neg_mean[:, r : r + 1],
                    in1=affine[:, 0, :],
                    op0=ALU.add,
                    op1=ALU.mult,
                )
            o_tiles[b] = o

        def normalise_and_store(b):
            rstd = stats[(b, "rstd")]
            tiles = SIZES[b] // P
            o = o_tiles[b]
            out_view = out_rows[STARTS[b] : STARTS[b] + SIZES[b], :].rearrange(
                "(p r) h -> p r h", p=P
            )
            for r in range(tiles):
                nc.vector.scalar_tensor_tensor(
                    out=o[:, r, :],
                    in0=o[:, r, :],
                    scalar=rstd[:, r : r + 1],
                    in1=affine[:, 1, :],
                    op0=ALU.mult,
                    op1=ALU.add,
                )
                nc.sync.dma_start(out=out_view[:, r, :], in_=o[:, r, :])

        def at(b, stage, *more):
            if 0 <= b < N_BLOCKS:
                stage(b, *more)

        for k in range(-4, N_BLOCKS + 1):
            at(k + 4, transpose_c)
            at(k + 3, quantise_c)
            at(k, quantise_h)
            at(k + 1, regroup_on_gpsimd)
            at(k + 1, regroup_on_vector)
            if k == -3:
                nc.vector.tensor_copy(out=b1[:], in_=b1_bf[:])
            at(k + 3, first_banks)
            at(k - 1, centre_and_scale)
            at(k + 2, relu_h, 0)
            at(k, second_product)
            at(k, add_bias)
            at(k + 2, relu_h, 1)
            at(k - 1, square_sums)
            if k == -3:
                prepare_w2()
            at(k + 2, relu_h, 2)
            at(k - 1, inverse_deviation)
            at(k + 2, relu_h, 3)
            if k == -2:
                prepare_vectors()
            at(k + 4, copy_c)
            at(k, mean)
            at(k - 1, normalise_and_store)
